import numpy as np
import ml_dtypes


BF16 = ml_dtypes.bfloat16


def bf(x):
    return np.asarray(x, np.float32).astype(BF16)


def f64(x):
    return np.asarray(x).astype(np.float64)


E2M1 = np.array([0.0, 0.5, 1.0, 1.5, 2.0, 3.0, 4.0, 6.0, -0.0, -0.5, -1.0, -1.5, -2.0, -3.0, -4.0, -6.0])


def pack_weight(w, fmt):
    k, n = w.shape
    w = f64(bf(w)).reshape(k // 32, 32, n)
    amax = np.abs(w).max(1)
    if fmt == "e4m3":
        byte = np.frexp(amax)[1] - 1 + 127 - 7
    else:
        mant, ex = np.frexp(amax / 6.0)
        byte = np.where(mant > 0.5, ex, ex - 1) + 127
    byte = np.clip(np.where(amax > 0, byte, 1), 1, 254)
    scaled = (w * np.exp2(127.0 - byte)[:, None, :]).reshape(k, n).astype(np.float32)
    by_word = np.ascontiguousarray(scaled.reshape(k // 512, 128, 4, n).transpose(0, 1, 3, 2))
    if fmt == "e4m3":
        words = by_word.astype(ml_dtypes.float8_e4m3fn).view(np.uint8)
    else:
        c = by_word.astype(ml_dtypes.float4_e2m1fn).view(np.uint8) & 0xF
        words = c[..., 0::2] | (c[..., 1::2] << 4)
    return np.ascontiguousarray(words), np.ascontiguousarray(byte.astype(np.uint8).reshape(k // 512, 16, n))


def unpack_weight(words, scales, fmt):
    g, p, n, _ = words.shape
    if fmt == "e4m3":
        vals = np.ascontiguousarray(words).view(ml_dtypes.float8_e4m3fn).astype(np.float64)
    else:
        nib = np.empty((g, p, n, 4), np.uint8)
        nib[..., 0::2] = words & 0xF
        nib[..., 1::2] = words >> 4
        vals = E2M1[nib]
    vals = vals * np.repeat(np.exp2(scales.astype(np.float64) - 127.0), 8, axis=1)[..., None]
    return vals.transpose(0, 1, 3, 2).reshape(g * 512, n)

def pack4(w):
    words, scales = pack_weight(w, "e2m1")
    return words.reshape(words.shape[0], 128, -1), scales


def unpack4(words, scales):
    return unpack_weight(words.reshape(words.shape[0], 128, -1, 2), scales, "e2m1")


def kspread(k):
    return np.exp2(np.repeat(np.random.randint(-6, 7, k // 32), 32).astype(np.float64))


B, T, H, HD = 2, 64, 16, 256
D = H * HD
HALF = HD // 2
ROPE_BASE = 10000.0


def to_heads(t):
    return t.reshape(B, T, H, HD).transpose(0, 2, 1, 3)


def rotate(t, cos, sin):
    t1, t2 = t[..., :HALF], t[..., HALF:]
    c = cos[None, None, :, :]
    s = sin[None, None, :, :]
    return np.concatenate([t1 * c - t2 * s, t1 * s + t2 * c], axis=-1)


def setup_inputs():
    s = kspread(D)
    inv_freq = 1.0 / (ROPE_BASE ** (np.arange(0, HD, 2) / HD))
    ang = np.arange(T)[:, None] * inv_freq[None, :]
    x = np.random.standard_normal((B, T, D)) * s
    x_words, x_scales = pack4(np.ascontiguousarray(x.reshape(B * T, D).T))
    Wqk = np.random.standard_normal((2 * D, D)) * D ** -0.5 / s[None, :]
    words, scales = pack4(np.ascontiguousarray(Wqk.T))
    return {"x_words": x_words,
            "x_scales": x_scales,
            "Wqk_words": words,
            "Wqk_scales": scales,
            "bqk": bf(np.random.standard_normal(2 * D) * 0.3),
            "cos": bf(np.cos(ang)),
            "sin": bf(np.sin(ang))}


def reference(x_words, x_scales, Wqk_words, Wqk_scales, bqk, cos, sin):
    xv = unpack4(x_words, x_scales).T.reshape(B, T, D)
    qk = (xv @ unpack4(Wqk_words, Wqk_scales)) + f64(bqk)
    q, k = np.split(qk, 2, axis=-1)
    q, k = to_heads(q), to_heads(k)
    return rotate(q, f64(cos), f64(sin)), rotate(k, f64(cos), f64(sin))

@@ -1,0 +1,213 @@
+from contextlib import ExitStack
+
+import concourse.mybir as mybir
+from concourse.masks import make_identity
+
+FLOPS = 2 * 128 * 4096 * 8192
+
+F32 = mybir.dt.float32
+BF16 = mybir.dt.bfloat16
+U8 = mybir.dt.uint8
+I32 = mybir.dt.int32
+FP4X4 = mybir.dt.float4_e2m1fn_x4
+ADD = mybir.AluOpType.add
+MULT = mybir.AluOpType.mult
+
+P = 128
+G = 8
+HD = 256
+HALF = 128
+BLK = 512
+CHUNK = 2048
+NBLK = 16
+SCALES_ON_GPSIMD = False
+HW_STORES = 1
+
+PLAN = [
+    [(0, 4, (2, 2, 2, 2))],
+    [(0, 4, (2, 2, 2, 2))],
+    [(0, 4, (2, 2, 2, 2))],
+    [(0, 2, (4, 4)), (2, 1, (8,)), (3, 1, (7, 1))],
+]
+
+
+def tile_selfattention_pa_kernel(
+    tc, x_words, x_scales, Wqk_words, Wqk_scales, bqk, cos, sin, out_0, out_1
+):
+    nc = tc.nc
+    with ExitStack() as ctx:
+        keep = ctx.enter_context(tc.tile_pool(name="keep", bufs=1))
+        wpool = ctx.enter_context(tc.tile_pool(name="wpool", bufs=3))
+        work = ctx.enter_context(tc.tile_pool(name="work", bufs=3))
+        psum = ctx.enter_context(tc.psum_pool(name="psum", bufs=8))
+        ctx.enter_context(tc.manual_schedule())
+
+        x_raw = keep.tile([P, G, 256], U8, name="x_raw", align_bytes=64)
+        x_codes = keep.tile([P, G, 256], U8, name="x_codes", align_bytes=64)
+        xs_raw = keep.tile([P, G, 128], U8, name="xs_raw", align_bytes=64)
+        xs = keep.tile([P, G, 128], U8, name="xs", align_bytes=64)
+        planes = [
+            keep.tile([P, G, CHUNK], U8, name="plane%d" % c, align_bytes=64) for c in range(4)
+        ]
+        ident = keep.tile([P, P], BF16, name="ident")
+        bias_rows = keep.tile([P, BLK], BF16, name="bias_rows")
+        bias_all = keep.tile([P, NBLK * BLK], BF16, name="bias_all")
+        cos_b = keep.tile([P, HALF], BF16, name="cos_b")
+        sin_b = keep.tile([P, HALF], BF16, name="sin_b")
+        cos2 = keep.tile([P, HD], F32, name="cos2")
+        sin2 = keep.tile([P, HD], F32, name="sin2")
+        wcs = [
+            wpool.tile([P, G, 2 * CHUNK], U8, name="wc%d" % c, tag="wc", align_bytes=64)
+            for c in range(4)
+        ]
+
+        def load_codes(c, blk0, nblk, g0, ng):
+            col0 = c * CHUNK + blk0 * BLK
+            nc.sync.dma_start(
+                out=wcs[c][:, g0 : g0 + ng, 2 * blk0 * BLK : 2 * (blk0 + nblk) * BLK].bitcast(I32),
+                in_=Wqk_words[g0 : g0 + ng, :, 2 * col0 : 2 * (col0 + nblk * BLK)]
+                .rearrange("g p n -> p g n")
+                .bitcast(I32),
+            )
+
+        def load_chunk_codes(c):
+            for blk0, nblk, split in PLAN[c]:
+                g0 = 0
+                for ng in split:
+                    load_codes(c, blk0, nblk, g0, ng)
+                    g0 += ng
+
+        def load_scales(c):
+            for r in range(4):
+                dst = planes[c][r:P:32, :, :]
+                src = Wqk_scales[:, r:16:4, c * CHUNK : (c + 1) * CHUNK].rearrange("g q n -> q g n")
+                if SCALES_ON_GPSIMD:
+                    nc.gpsimd.dma_start(out=dst.bitcast(F32), in_=src.bitcast(F32))
+                else:
+                    nc.sync.dma_start(out=dst.bitcast(I32), in_=src.bitcast(I32))
+
+        def spread_bias(j):
+            bp = psum.tile([P, BLK], F32, name="bp%d" % j, tag="acc")
+            nc.tensor.matmul(
+                out=bp[:],
+                lhsT=ident[:, j : j + 1].to_broadcast([P, P]),
+                rhs=bias_rows[:],
+                start=True,
+                stop=True,
+            )
+            nc.scalar.copy(out=bias_all[:, j * BLK : (j + 1) * BLK], in_=bp[:])
+
+        def epilogue(j, acc):
+            t = work.tile([P, BLK], F32, name="t%d" % j, tag="t")
+            u = work.tile([P, BLK], F32, name="u%d" % j, tag="u")
+            w = work.tile([P, BLK], F32, name="w%d" % j, tag="w")
+            o = work.tile([P, BLK], F32, name="o%d" % j, tag="o")
+            for h in range(2):
+                a = h * HD
+                nc.vector.tensor_tensor(
+                    out=t[:, a : a + HD],
+                    in0=acc[:, a : a + HD],
+                    in1=bias_all[:, j * BLK + a : j * BLK + a + HD],
+                    op=ADD,
+                )
+            for h in range(2):
+                a = h * HD
+                nc.vector.tensor_tensor(out=u[:, a : a + HD], in0=t[:, a : a + HD], in1=cos2[:], op=MULT)
+                nc.vector.tensor_tensor(out=w[:, a : a + HD], in0=t[:, a : a + HD], in1=sin2[:], op=MULT)
+            for h in range(2):
+                a = h * HD
+                m = a + HALF
+                nc.vector.tensor_tensor(out=o[:, a:m], in0=u[:, a:m], in1=w[:, m : a + HD], op=ADD)
+                nc.vector.tensor_tensor(out=o[:, m : a + HD], in0=u[:, m : a + HD], in1=w[:, a:m], op=ADD)
+            dst = out_0 if j < 8 else out_1
+            h0 = (j % 8) * 2
+            queue = nc.scalar if j >= NBLK - HW_STORES else nc.gpsimd
+            for b in range(2):
+                queue.dma_start(
+                    out=dst[b, h0 : h0 + 2, :, :].rearrange("h t f -> t h f"),
+                    in_=o[b:P:2, :].rearrange("p (h f) -> p h f", h=2),
+                )
+
+        nc.vector.memset(xs_raw[:].bitcast(I32), 0)
+        nc.vector.memset(planes[0][:].bitcast(I32), 0)
+        nc.vector.memset(planes[1][:].bitcast(I32), 0)
+        nc.gpsimd.memset(bias_rows[:], 0.0)
+        nc.gpsimd.dma_start(out=bias_rows[0:16, :], in_=bqk.rearrange("(j n) -> j n", j=16))
+        make_identity(nc, ident[:])
+
+        load_codes(0, 0, 4, 0, 2)
+        nc.sync.dma_start(
+            out=x_raw[:].bitcast(I32), in_=x_words.rearrange("g p n -> p g n").bitcast(I32)
+        )
+        for r in range(4):
+            nc.sync.dma_start(
+                out=xs_raw[r:P:32, :, :].bitcast(I32),
+                in_=x_scales[:, r:16:4, :].rearrange("g q n -> q g n").bitcast(I32),
+            )
+        load_scales(0)
+        for g0 in (2, 4, 6):
+            load_codes(0, 0, 4, g0, 2)
+        for b in range(2):
+            nc.gpsimd.dma_start(out=cos_b[b:P:2, :], in_=cos)
+            nc.gpsimd.dma_start(out=sin_b[b:P:2, :], in_=sin)
+        load_scales(1)
+        load_chunk_codes(1)
+
+        for g in range(G):
+            nc.vector.tensor_copy(
+                out=x_codes[:, g, :].rearrange("p (t b w) -> p t b w", b=2, w=2),
+                in_=x_raw[:, g, :].rearrange("p (b t w) -> p t b w", b=2, w=2),
+            )
+        nc.vector.tensor_copy(
+            out=xs[:].rearrange("p g (t b) -> p g t b", b=2),
+            in_=xs_raw[:].rearrange("p g (b t) -> p g t b", b=2),
+        )
+        nc.gpsimd.memset(planes[2][:].bitcast(F32), 0.0)
+        nc.gpsimd.tensor_copy(out=cos2[:, 0:HALF], in_=cos_b[:])
+        nc.gpsimd.tensor_copy(out=cos2[:, HALF:HD], in_=cos_b[:])
+        nc.gpsimd.tensor_copy(out=sin2[:, 0:HALF], in_=sin_b[:])
+        nc.gpsimd.tensor_scalar(
+            out=sin2[:, HALF:HD], in0=sin_b[:], scalar1=-1.0, scalar2=0.0, op0=MULT, op1=ADD
+        )
+        nc.gpsimd.memset(planes[3][:].bitcast(F32), 0.0)
+        if not SCALES_ON_GPSIMD:
+            for c in (2, 3):
+                load_scales(c)
+                load_chunk_codes(c)
+        else:
+            load_chunk_codes(2)
+            load_chunk_codes(3)
+
+        for j in range(8):
+            spread_bias(j)
+
+        for c in range(4):
+            first = True
+            for blk0, nblk, split in PLAN[c]:
+                accs = [
+                    psum.tile([P, BLK], F32, name="acc%d_%d" % (c, blk0 + i), tag="acc")
+                    for i in range(nblk)
+                ]
+                g0 = 0
+                for ng in split:
+                    for i in range(nblk):
+                        blk = blk0 + i
+                        for g in range(g0, g0 + ng):
+                            nc.tensor.matmul_mx(
+                                out=accs[i][:],
+                                lhsT=x_codes[:, g, :].bitcast(FP4X4),
+                                lhsT_scale=xs[:, g, :],
+                                rhs=wcs[c][:, g, 2 * blk * BLK : 2 * (blk + 1) * BLK].bitcast(FP4X4),
+                                rhs_scale=planes[c][:, g, blk * BLK : (blk + 1) * BLK],
+                                start=(g == 0),
+                                stop=(g == G - 1),
+                            )
+                    g0 += ng
+                if c == 0:
+                    for j in range(8, NBLK):
+                        spread_bias(j)
+                for i in range(nblk):
+                    epilogue(c * 4 + blk0 + i, accs[i])
+                    if SCALES_ON_GPSIMD and first and c < 2:
+                        load_scales(c + 2)
+                    first = False

@@ -21,7 +21,6 @@ BLK = 512
 CHUNK = 2048
 NBLK = 16
 SCALES_ON_GPSIMD = False
-HW_STORES = 1
 
 PLAN = [
     [(0, 4, (2, 2, 2, 2))],
@@ -70,21 +69,27 @@ def tile_selfattention_pa_kernel(
                 .bitcast(I32),
             )
 
-        def load_chunk_codes(c):
+        def load_scales(c, r):
+            dst = planes[c][r:P:32, :, :]
+            src = Wqk_scales[:, r:16:4, c * CHUNK : (c + 1) * CHUNK].rearrange("g q n -> q g n")
+            if SCALES_ON_GPSIMD:
+                nc.gpsimd.dma_start(out=dst.bitcast(F32), in_=src.bitcast(F32))
+            else:
+                nc.sync.dma_start(out=dst.bitcast(I32), in_=src.bitcast(I32))
+
+        def chunk_loads(c):
+            todo = [(load_scales, (c, r)) for r in range(4)]
             for blk0, nblk, split in PLAN[c]:
                 g0 = 0
                 for ng in split:
-                    load_codes(c, blk0, nblk, g0, ng)
+                    todo.append((load_codes, (c, blk0, nblk, g0, ng)))
                     g0 += ng
+            return todo
 
-        def load_scales(c):
-            for r in range(4):
-                dst = planes[c][r:P:32, :, :]
-                src = Wqk_scales[:, r:16:4, c * CHUNK : (c + 1) * CHUNK].rearrange("g q n -> q g n")
-                if SCALES_ON_GPSIMD:
-                    nc.gpsimd.dma_start(out=dst.bitcast(F32), in_=src.bitcast(F32))
-                else:
-                    nc.sync.dma_start(out=dst.bitcast(I32), in_=src.bitcast(I32))
+        def issue(todo, n):
+            for fn, args in todo[:n]:
+                fn(*args)
+            return todo[n:]
 
         def spread_bias(j):
             bp = psum.tile([P, BLK], F32, name="bp%d" % j, tag="acc")
@@ -101,7 +106,7 @@ def tile_selfattention_pa_kernel(
             t = work.tile([P, BLK], F32, name="t%d" % j, tag="t")
             u = work.tile([P, BLK], F32, name="u%d" % j, tag="u")
             w = work.tile([P, BLK], F32, name="w%d" % j, tag="w")
-            o = work.tile([P, BLK], F32, name="o%d" % j, tag="o")
+            o = work.tile([P, BLK], F32, name="o%d" % j, tag="o", bufs=10)
             for h in range(2):
                 a = h * HD
                 nc.vector.tensor_tensor(
@@ -119,11 +124,13 @@ def tile_selfattention_pa_kernel(
                 m = a + HALF
                 nc.vector.tensor_tensor(out=o[:, a:m], in0=u[:, a:m], in1=w[:, m : a + HD], op=ADD)
                 nc.vector.tensor_tensor(out=o[:, m : a + HD], in0=u[:, m : a + HD], in1=w[:, a:m], op=ADD)
+            return o
+
+        def store(j, o):
             dst = out_0 if j < 8 else out_1
             h0 = (j % 8) * 2
-            queue = nc.scalar if j >= NBLK - HW_STORES else nc.gpsimd
             for b in range(2):
-                queue.dma_start(
+                nc.sync.dma_start(
                     out=dst[b, h0 : h0 + 2, :, :].rearrange("h t f -> t h f"),
                     in_=o[b:P:2, :].rearrange("p (h f) -> p h f", h=2),
                 )
@@ -144,14 +151,14 @@ def tile_selfattention_pa_kernel(
                 out=xs_raw[r:P:32, :, :].bitcast(I32),
                 in_=x_scales[:, r:16:4, :].rearrange("g q n -> q g n").bitcast(I32),
             )
-        load_scales(0)
+        for r in range(4):
+            load_scales(0, r)
         for g0 in (2, 4, 6):
             load_codes(0, 0, 4, g0, 2)
         for b in range(2):
             nc.gpsimd.dma_start(out=cos_b[b:P:2, :], in_=cos)
             nc.gpsimd.dma_start(out=sin_b[b:P:2, :], in_=sin)
-        load_scales(1)
-        load_chunk_codes(1)
+        issue(chunk_loads(1), 99)
 
         for g in range(G):
             nc.vector.tensor_copy(
@@ -170,19 +177,14 @@ def tile_selfattention_pa_kernel(
             out=sin2[:, HALF:HD], in0=sin_b[:], scalar1=-1.0, scalar2=0.0, op0=MULT, op1=ADD
         )
         nc.gpsimd.memset(planes[3][:].bitcast(F32), 0.0)
-        if not SCALES_ON_GPSIMD:
-            for c in (2, 3):
-                load_scales(c)
-                load_chunk_codes(c)
-        else:
-            load_chunk_codes(2)
-            load_chunk_codes(3)
 
         for j in range(8):
             spread_bias(j)
+        late_bias = list(range(8, NBLK))
 
         for c in range(4):
-            first = True
+            todo = chunk_loads(c + 2) if c + 2 < 4 else []
+            done = []
             for blk0, nblk, split in PLAN[c]:
                 accs = [
                     psum.tile([P, BLK], F32, name="acc%d_%d" % (c, blk0 + i), tag="acc")
@@ -203,11 +205,16 @@ def tile_selfattention_pa_kernel(
                                 stop=(g == G - 1),
                             )
                     g0 += ng
-                if c == 0:
-                    for j in range(8, NBLK):
+                    for j in late_bias[:3]:
                         spread_bias(j)
+                    late_bias = late_bias[3:]
                 for i in range(nblk):
-                    epilogue(c * 4 + blk0 + i, accs[i])
-                    if SCALES_ON_GPSIMD and first and c < 2:
-                        load_scales(c + 2)
-                    first = False
+                    j = c * 4 + blk0 + i
+                    done.append((j, epilogue(j, accs[i])))
+                    if not todo:
+                        store(*done.pop())
+            todo = issue(todo, 4)
+            for j, o in done:
+                todo = issue(todo, 1)
+                store(j, o)
+            issue(todo, 99)

@@ -78,7 +78,7 @@ def tile_selfattention_pa_kernel(
                 nc.sync.dma_start(out=dst.bitcast(I32), in_=src.bitcast(I32))
 
         def chunk_loads(c):
-            todo = [(load_scales, (c, r)) for r in range(4)]
+            todo = []
             for blk0, nblk, split in PLAN[c]:
                 g0 = 0
                 for ng in split:
@@ -136,28 +136,30 @@ def tile_selfattention_pa_kernel(
                 )
 
         nc.vector.memset(xs_raw[:].bitcast(I32), 0)
-        nc.vector.memset(planes[0][:].bitcast(I32), 0)
-        nc.vector.memset(planes[1][:].bitcast(I32), 0)
+        for c in range(3):
+            nc.vector.memset(planes[c][:].bitcast(I32), 0)
         nc.gpsimd.memset(bias_rows[:], 0.0)
         nc.gpsimd.dma_start(out=bias_rows[0:16, :], in_=bqk.rearrange("(j n) -> j n", j=16))
+        nc.gpsimd.memset(planes[3][:].bitcast(F32), 0.0)
         make_identity(nc, ident[:])
+        for b in range(2):
+            nc.gpsimd.dma_start(out=cos_b[b:P:2, :], in_=cos)
+            nc.gpsimd.dma_start(out=sin_b[b:P:2, :], in_=sin)
 
-        load_codes(0, 0, 4, 0, 2)
-        nc.sync.dma_start(
-            out=x_raw[:].bitcast(I32), in_=x_words.rearrange("g p n -> p g n").bitcast(I32)
-        )
+        for c in range(4):
+            for r in range(4):
+                load_scales(c, r)
         for r in range(4):
             nc.sync.dma_start(
                 out=xs_raw[r:P:32, :, :].bitcast(I32),
                 in_=x_scales[:, r:16:4, :].rearrange("g q n -> q g n").bitcast(I32),
             )
-        for r in range(4):
-            load_scales(0, r)
-        for g0 in (2, 4, 6):
-            load_codes(0, 0, 4, g0, 2)
-        for b in range(2):
-            nc.gpsimd.dma_start(out=cos_b[b:P:2, :], in_=cos)
-            nc.gpsimd.dma_start(out=sin_b[b:P:2, :], in_=sin)
+        for g0, g1 in ((0, 3), (3, 6), (6, 8)):
+            nc.sync.dma_start(
+                out=x_raw[:, g0:g1, :].bitcast(I32),
+                in_=x_words[g0:g1, :, :].rearrange("g p n -> p g n").bitcast(I32),
+            )
+        issue(chunk_loads(0), 99)
         issue(chunk_loads(1), 99)
 
         for g in range(G):
@@ -169,18 +171,16 @@ def tile_selfattention_pa_kernel(
             out=xs[:].rearrange("p g (t b) -> p g t b", b=2),
             in_=xs_raw[:].rearrange("p g (b t) -> p g t b", b=2),
         )
-        nc.gpsimd.memset(planes[2][:].bitcast(F32), 0.0)
         nc.gpsimd.tensor_copy(out=cos2[:, 0:HALF], in_=cos_b[:])
         nc.gpsimd.tensor_copy(out=cos2[:, HALF:HD], in_=cos_b[:])
         nc.gpsimd.tensor_copy(out=sin2[:, 0:HALF], in_=sin_b[:])
         nc.gpsimd.tensor_scalar(
             out=sin2[:, HALF:HD], in0=sin_b[:], scalar1=-1.0, scalar2=0.0, op0=MULT, op1=ADD
         )
-        nc.gpsimd.memset(planes[3][:].bitcast(F32), 0.0)
 
-        for j in range(8):
+        for j in range(NBLK):
             spread_bias(j)
-        late_bias = list(range(8, NBLK))
+        late_bias = []
 
         for c in range(4):
             todo = chunk_loads(c + 2) if c + 2 < 4 else []
@@ -213,7 +213,6 @@ def tile_selfattention_pa_kernel(
                     done.append((j, epilogue(j, accs[i])))
                     if not todo:
                         store(*done.pop())
-            todo = issue(todo, 4)
             for j, o in done:
                 todo = issue(todo, 1)
                 store(j, o)

@@ -20,7 +20,7 @@ HALF = 128
 BLK = 512
 CHUNK = 2048
 NBLK = 16
-SCALES_ON_GPSIMD = False
+FILL = 5
 
 PLAN = [
     [(0, 4, (2, 2, 2, 2))],
@@ -46,7 +46,7 @@ def tile_selfattention_pa_kernel(
         xs_raw = keep.tile([P, G, 128], U8, name="xs_raw", align_bytes=64)
         xs = keep.tile([P, G, 128], U8, name="xs", align_bytes=64)
         planes = [
-            keep.tile([P, G, CHUNK], U8, name="plane%d" % c, align_bytes=64) for c in range(4)
+            keep.tile([P, G, CHUNK], U8, name="plane%d" % c, align_bytes=64) for c in range(2)
         ]
         ident = keep.tile([P, P], BF16, name="ident")
         bias_rows = keep.tile([P, BLK], BF16, name="bias_rows")
@@ -69,27 +69,23 @@ def tile_selfattention_pa_kernel(
                 .bitcast(I32),
             )
 
-        def load_scales(c, r):
-            dst = planes[c][r:P:32, :, :]
-            src = Wqk_scales[:, r:16:4, c * CHUNK : (c + 1) * CHUNK].rearrange("g q n -> q g n")
-            if SCALES_ON_GPSIMD:
-                nc.gpsimd.dma_start(out=dst.bitcast(F32), in_=src.bitcast(F32))
-            else:
-                nc.sync.dma_start(out=dst.bitcast(I32), in_=src.bitcast(I32))
+        def load_scales(c):
+            cols = slice(c * CHUNK, (c + 1) * CHUNK)
+            for q in range(2):
+                for r in range(4):
+                    nc.sync.dma_start(
+                        out=planes[c % 2][32 * q + r : P : 64, :, :].bitcast(I32),
+                        in_=Wqk_scales[:, 4 * q + r : 16 : 8, cols].rearrange("g q n -> q g n").bitcast(I32),
+                    )
 
-        def chunk_loads(c):
+        def code_loads(c):
             todo = []
             for blk0, nblk, split in PLAN[c]:
                 g0 = 0
                 for ng in split:
-                    todo.append((load_codes, (c, blk0, nblk, g0, ng)))
+                    todo.append((c, blk0, nblk, g0, ng))
                     g0 += ng
             return todo
-
-        def issue(todo, n):
-            for fn, args in todo[:n]:
-                fn(*args)
-            return todo[n:]
 
         def spread_bias(j):
             bp = psum.tile([P, BLK], F32, name="bp%d" % j, tag="acc")
@@ -106,7 +102,7 @@ def tile_selfattention_pa_kernel(
             t = work.tile([P, BLK], F32, name="t%d" % j, tag="t")
             u = work.tile([P, BLK], F32, name="u%d" % j, tag="u")
             w = work.tile([P, BLK], F32, name="w%d" % j, tag="w")
-            o = work.tile([P, BLK], F32, name="o%d" % j, tag="o", bufs=10)
+            o = work.tile([P, BLK], F32, name="o%d" % j, tag="o", bufs=12)
             for h in range(2):
                 a = h * HD
                 nc.vector.tensor_tensor(
@@ -126,41 +122,40 @@ def tile_selfattention_pa_kernel(
                 nc.vector.tensor_tensor(out=o[:, m : a + HD], in0=u[:, m : a + HD], in1=w[:, a:m], op=ADD)
             return o
 
-        def store(j, o):
+        def store(j, o, b):
             dst = out_0 if j < 8 else out_1
             h0 = (j % 8) * 2
-            for b in range(2):
-                nc.sync.dma_start(
-                    out=dst[b, h0 : h0 + 2, :, :].rearrange("h t f -> t h f"),
-                    in_=o[b:P:2, :].rearrange("p (h f) -> p h f", h=2),
-                )
+            nc.sync.dma_start(
+                out=dst[b, h0 : h0 + 2, :, :].rearrange("h t f -> t h f"),
+                in_=o[b:P:2, :].rearrange("p (h f) -> p h f", h=2),
+            )
 
         nc.vector.memset(xs_raw[:].bitcast(I32), 0)
-        for c in range(3):
-            nc.vector.memset(planes[c][:].bitcast(I32), 0)
+        nc.vector.memset(planes[0][:].bitcast(I32), 0)
+        nc.vector.memset(planes[1][:].bitcast(I32), 0)
         nc.gpsimd.memset(bias_rows[:], 0.0)
-        nc.gpsimd.dma_start(out=bias_rows[0:16, :], in_=bqk.rearrange("(j n) -> j n", j=16))
-        nc.gpsimd.memset(planes[3][:].bitcast(F32), 0.0)
         make_identity(nc, ident[:])
-        for b in range(2):
-            nc.gpsimd.dma_start(out=cos_b[b:P:2, :], in_=cos)
-            nc.gpsimd.dma_start(out=sin_b[b:P:2, :], in_=sin)
 
-        for c in range(4):
-            for r in range(4):
-                load_scales(c, r)
-        for r in range(4):
-            nc.sync.dma_start(
-                out=xs_raw[r:P:32, :, :].bitcast(I32),
-                in_=x_scales[:, r:16:4, :].rearrange("g q n -> q g n").bitcast(I32),
-            )
+        first = code_loads(0)
+        load_codes(*first[0])
         for g0, g1 in ((0, 3), (3, 6), (6, 8)):
             nc.sync.dma_start(
                 out=x_raw[:, g0:g1, :].bitcast(I32),
                 in_=x_words[g0:g1, :, :].rearrange("g p n -> p g n").bitcast(I32),
             )
-        issue(chunk_loads(0), 99)
-        issue(chunk_loads(1), 99)
+        for r in range(4):
+            nc.sync.dma_start(
+                out=xs_raw[r:P:32, :, :].bitcast(I32),
+                in_=x_scales[:, r:16:4, :].rearrange("g q n -> q g n").bitcast(I32),
+            )
+        load_scales(0)
+        load_scales(1)
+        nc.sync.dma_start(out=bias_rows[0:16, :], in_=bqk.rearrange("(j n) -> j n", j=16))
+        for b in range(2):
+            nc.sync.dma_start(out=cos_b[b:P:2, :], in_=cos)
+            nc.sync.dma_start(out=sin_b[b:P:2, :], in_=sin)
+        for args in first[1:] + code_loads(1):
+            load_codes(*args)
 
         for g in range(G):
             nc.vector.tensor_copy(
@@ -178,13 +173,10 @@ def tile_selfattention_pa_kernel(
             out=sin2[:, HALF:HD], in0=sin_b[:], scalar1=-1.0, scalar2=0.0, op0=MULT, op1=ADD
         )
 
-        for j in range(NBLK):
-            spread_bias(j)
-        late_bias = []
+        bias_todo = list(range(NBLK))
+        waiting = []
 
         for c in range(4):
-            todo = chunk_loads(c + 2) if c + 2 < 4 else []
-            done = []
             for blk0, nblk, split in PLAN[c]:
                 accs = [
                     psum.tile([P, BLK], F32, name="acc%d_%d" % (c, blk0 + i), tag="acc")
@@ -200,20 +192,34 @@ def tile_selfattention_pa_kernel(
                                 lhsT=x_codes[:, g, :].bitcast(FP4X4),
                                 lhsT_scale=xs[:, g, :],
                                 rhs=wcs[c][:, g, 2 * blk * BLK : 2 * (blk + 1) * BLK].bitcast(FP4X4),
-                                rhs_scale=planes[c][:, g, blk * BLK : (blk + 1) * BLK],
+                                rhs_scale=planes[c % 2][:, g, blk * BLK : (blk + 1) * BLK],
                                 start=(g == 0),
                                 stop=(g == G - 1),
                             )
                     g0 += ng
-                    for j in late_bias[:3]:
+                    for j in bias_todo[:4]:
                         spread_bias(j)
-                    late_bias = late_bias[3:]
+                    bias_todo = bias_todo[4:]
                 for i in range(nblk):
                     j = c * 4 + blk0 + i
-                    done.append((j, epilogue(j, accs[i])))
-                    if not todo:
-                        store(*done.pop())
-            for j, o in done:
-                todo = issue(todo, 1)
-                store(j, o)
-            issue(todo, 99)
+                    o = epilogue(j, accs[i])
+                    waiting.extend([(j, o, 0), (j, o, 1)])
+            if c < 2:
+                load_scales(c + 2)
+                for args in waiting[:FILL]:
+                    store(*args)
+                waiting = waiting[FILL:]
+                todo = code_loads(c + 2)
+                if c == 0:
+                    for args in todo[:3]:
+                        load_codes(*args)
+                    store(*waiting[0])
+                    load_codes(*todo[3])
+                    for args in waiting[1:]:
+                        store(*args)
+                    waiting = []
+                else:
+                    for args in todo:
+                        load_codes(*args)
+        for args in waiting:
+            store(*args)

@@ -137,7 +137,6 @@ def tile_selfattention_pa_kernel(
         make_identity(nc, ident[:])
 
         first = code_loads(0)
-        load_codes(*first[0])
         for g0, g1 in ((0, 3), (3, 6), (6, 8)):
             nc.sync.dma_start(
                 out=x_raw[:, g0:g1, :].bitcast(I32),
@@ -148,6 +147,7 @@ def tile_selfattention_pa_kernel(
                 out=xs_raw[r:P:32, :, :].bitcast(I32),
                 in_=x_scales[:, r:16:4, :].rearrange("g q n -> q g n").bitcast(I32),
             )
+        load_codes(*first[0])
         load_scales(0)
         load_scales(1)
         nc.sync.dma_start(out=bias_rows[0:16, :], in_=bqk.rearrange("(j n) -> j n", j=16))

@@ -148,13 +148,14 @@ def tile_selfattention_pa_kernel(
                 in_=x_scales[:, r:16:4, :].rearrange("g q n -> q g n").bitcast(I32),
             )
         load_codes(*first[0])
+        load_codes(*first[1])
         load_scales(0)
         load_scales(1)
         nc.sync.dma_start(out=bias_rows[0:16, :], in_=bqk.rearrange("(j n) -> j n", j=16))
         for b in range(2):
             nc.sync.dma_start(out=cos_b[b:P:2, :], in_=cos)
             nc.sync.dma_start(out=sin_b[b:P:2, :], in_=sin)
-        for args in first[1:] + code_loads(1):
+        for args in first[2:] + code_loads(1):
             load_codes(*args)
 
         for g in range(G):

@@ -210,17 +210,7 @@ def tile_selfattention_pa_kernel(
                 for args in waiting[:FILL]:
                     store(*args)
                 waiting = waiting[FILL:]
-                todo = code_loads(c + 2)
-                if c == 0:
-                    for args in todo[:3]:
-                        load_codes(*args)
-                    store(*waiting[0])
-                    load_codes(*todo[3])
-                    for args in waiting[1:]:
-                        store(*args)
-                    waiting = []
-                else:
-                    for args in todo:
-                        load_codes(*args)
+                for args in code_loads(c + 2):
+                    load_codes(*args)
         for args in waiting:
             store(*args)

@@ -26,7 +26,7 @@ PLAN = [
     [(0, 4, (2, 2, 2, 2))],
     [(0, 4, (2, 2, 2, 2))],
     [(0, 4, (2, 2, 2, 2))],
-    [(0, 2, (4, 4)), (2, 1, (8,)), (3, 1, (7, 1))],
+    [(0, 2, (4, 2, 2)), (2, 1, (4, 4)), (3, 1, (4, 3, 1))],
 ]
 
 
@@ -53,8 +53,10 @@ def tile_selfattention_pa_kernel(
         bias_all = keep.tile([P, NBLK * BLK], BF16, name="bias_all")
         cos_b = keep.tile([P, HALF], BF16, name="cos_b")
         sin_b = keep.tile([P, HALF], BF16, name="sin_b")
-        cos2 = keep.tile([P, HD], F32, name="cos2")
-        sin2 = keep.tile([P, HD], F32, name="sin2")
+        cos4 = keep.tile([P, BLK], F32, name="cos4")
+        sin4 = keep.tile([P, BLK], F32, name="sin4")
+        cos2 = cos4[:, 0:HD]
+        sin2 = sin4[:, 0:HD]
         wcs = [
             wpool.tile([P, G, 2 * CHUNK], U8, name="wc%d" % c, tag="wc", align_bytes=64)
             for c in range(4)
@@ -113,14 +115,45 @@ def tile_selfattention_pa_kernel(
                 )
             for h in range(2):
                 a = h * HD
-                nc.vector.tensor_tensor(out=u[:, a : a + HD], in0=t[:, a : a + HD], in1=cos2[:], op=MULT)
-                nc.vector.tensor_tensor(out=w[:, a : a + HD], in0=t[:, a : a + HD], in1=sin2[:], op=MULT)
+                nc.vector.tensor_tensor(out=u[:, a : a + HD], in0=t[:, a : a + HD], in1=cos2, op=MULT)
+                nc.vector.tensor_tensor(out=w[:, a : a + HD], in0=t[:, a : a + HD], in1=sin2, op=MULT)
             for h in range(2):
                 a = h * HD
                 m = a + HALF
                 nc.vector.tensor_tensor(out=o[:, a:m], in0=u[:, a:m], in1=w[:, m : a + HD], op=ADD)
                 nc.vector.tensor_tensor(out=o[:, m : a + HD], in0=u[:, m : a + HD], in1=w[:, a:m], op=ADD)
             return o
+
+        def epilogue_pair(j, acc_a, acc_b):
+            tiles = []
+            for i in range(2):
+                tiles.append(
+                    (
+                        work.tile([P, BLK], F32, name="t%d" % (j + i), tag="t"),
+                        work.tile([P, BLK], F32, name="u%d" % (j + i), tag="u"),
+                        work.tile([P, BLK], F32, name="w%d" % (j + i), tag="w"),
+                        work.tile([P, BLK], F32, name="o%d" % (j + i), tag="o", bufs=12),
+                    )
+                )
+            for i, acc in enumerate((acc_a, acc_b)):
+                nc.vector.tensor_tensor(
+                    out=tiles[i][0][:],
+                    in0=acc[:],
+                    in1=bias_all[:, (j + i) * BLK : (j + i + 1) * BLK],
+                    op=ADD,
+                )
+            for i in range(2):
+                t, u, w, o = tiles[i]
+                nc.vector.tensor_tensor(out=u[:], in0=t[:], in1=cos4[:], op=MULT)
+                nc.vector.tensor_tensor(out=w[:], in0=t[:], in1=sin4[:], op=MULT)
+            for i in range(2):
+                t, u, w, o = tiles[i]
+                o3 = o[:].rearrange("p (h f) -> p h f", h=2)
+                u3 = u[:].rearrange("p (h f) -> p h f", h=2)
+                w3 = w[:].rearrange("p (h f) -> p h f", h=2)
+                nc.vector.tensor_tensor(out=o3[:, :, 0:HALF], in0=u3[:, :, 0:HALF], in1=w3[:, :, HALF:HD], op=ADD)
+                nc.vector.tensor_tensor(out=o3[:, :, HALF:HD], in0=u3[:, :, HALF:HD], in1=w3[:, :, 0:HALF], op=ADD)
+            return tiles[0][3], tiles[1][3]
 
         def store(j, o, b):
             dst = out_0 if j < 8 else out_1
@@ -167,12 +200,13 @@ def tile_selfattention_pa_kernel(
             out=xs[:].rearrange("p g (t b) -> p g t b", b=2),
             in_=xs_raw[:].rearrange("p g (b t) -> p g t b", b=2),
         )
-        nc.gpsimd.tensor_copy(out=cos2[:, 0:HALF], in_=cos_b[:])
-        nc.gpsimd.tensor_copy(out=cos2[:, HALF:HD], in_=cos_b[:])
-        nc.gpsimd.tensor_copy(out=sin2[:, 0:HALF], in_=sin_b[:])
-        nc.gpsimd.tensor_scalar(
-            out=sin2[:, HALF:HD], in0=sin_b[:], scalar1=-1.0, scalar2=0.0, op0=MULT, op1=ADD
-        )
+        for a in range(0, BLK, HD):
+            nc.gpsimd.tensor_copy(out=cos4[:, a : a + HALF], in_=cos_b[:])
+            nc.gpsimd.tensor_copy(out=cos4[:, a + HALF : a + HD], in_=cos_b[:])
+            nc.gpsimd.tensor_copy(out=sin4[:, a : a + HALF], in_=sin_b[:])
+            nc.gpsimd.tensor_scalar(
+                out=sin4[:, a + HALF : a + HD], in0=sin_b[:], scalar1=-1.0, scalar2=0.0, op0=MULT, op1=ADD
+            )
 
         bias_todo = list(range(NBLK))
         waiting = []
@@ -201,10 +235,13 @@ def tile_selfattention_pa_kernel(
                     for j in bias_todo[:4]:
                         spread_bias(j)
                     bias_todo = bias_todo[4:]
+                j = c * 4 + blk0
+                if nblk == 2:
+                    done = epilogue_pair(j, accs[0], accs[1])
+                else:
+                    done = [epilogue(j + i, accs[i]) for i in range(nblk)]
                 for i in range(nblk):
-                    j = c * 4 + blk0 + i
-                    o = epilogue(j, accs[i])
-                    waiting.extend([(j, o, 0), (j, o, 1)])
+                    waiting.extend([(j + i, done[i], 0), (j + i, done[i], 1)])
             if c < 2:
                 load_scales(c + 2)
                 for args in waiting[:FILL]:

@@ -26,7 +26,7 @@ PLAN = [
     [(0, 4, (2, 2, 2, 2))],
     [(0, 4, (2, 2, 2, 2))],
     [(0, 4, (2, 2, 2, 2))],
-    [(0, 2, (4, 2, 2)), (2, 1, (4, 4)), (3, 1, (4, 3, 1))],
+    [(0, 2, (4, 2, 2)), (2, 2, (4, 3, 1))],
 ]
 
 

@@ -25,8 +25,8 @@ FILL = 5
 PLAN = [
     [(0, 4, (2, 2, 2, 2))],
     [(0, 4, (2, 2, 2, 2))],
-    [(0, 4, (2, 2, 2, 2))],
-    [(0, 2, (4, 2, 2)), (2, 2, (4, 3, 1))],
+    [(0, 4, (2, 2, 2, 1, 1))],
+    [(0, 2, (4, 3, 1)), (2, 2, (4, 3, 1))],
 ]
 
 
@@ -236,8 +236,10 @@ def tile_selfattention_pa_kernel(
                         spread_bias(j)
                     bias_todo = bias_todo[4:]
                 j = c * 4 + blk0
-                if nblk == 2:
-                    done = epilogue_pair(j, accs[0], accs[1])
+                if c >= 2:
+                    done = []
+                    for i in range(0, nblk, 2):
+                        done.extend(epilogue_pair(j + i, accs[i], accs[i + 1]))
                 else:
                     done = [epilogue(j + i, accs[i]) for i in range(nblk)]
                 for i in range(nblk):

from contextlib import ExitStack

import concourse.mybir as mybir
from concourse.masks import make_identity

FLOPS = 2 * 128 * 4096 * 8192

F32 = mybir.dt.float32
BF16 = mybir.dt.bfloat16
U8 = mybir.dt.uint8
I32 = mybir.dt.int32
FP4X4 = mybir.dt.float4_e2m1fn_x4
ADD = mybir.AluOpType.add
MULT = mybir.AluOpType.mult

P = 128
G = 8
HD = 256
HALF = 128
BLK = 512
CHUNK = 2048
NBLK = 16
FILL = 5

PLAN = [
    [(0, 4, (2, 2, 2, 2))],
    [(0, 4, (2, 2, 2, 2))],
    [(0, 4, (2, 2, 2, 1, 1))],
    [(0, 2, (4, 3, 1)), (2, 2, (4, 3, 1))],
]


def tile_selfattention_pa_kernel(
    tc, x_words, x_scales, Wqk_words, Wqk_scales, bqk, cos, sin, out_0, out_1
):
    nc = tc.nc
    with ExitStack() as ctx:
        keep = ctx.enter_context(tc.tile_pool(name="keep", bufs=1))
        wpool = ctx.enter_context(tc.tile_pool(name="wpool", bufs=3))
        work = ctx.enter_context(tc.tile_pool(name="work", bufs=3))
        psum = ctx.enter_context(tc.psum_pool(name="psum", bufs=8))
        ctx.enter_context(tc.manual_schedule())

        x_raw = keep.tile([P, G, 256], U8, name="x_raw", align_bytes=64)
        x_codes = keep.tile([P, G, 256], U8, name="x_codes", align_bytes=64)
        xs_raw = keep.tile([P, G, 128], U8, name="xs_raw", align_bytes=64)
        xs = keep.tile([P, G, 128], U8, name="xs", align_bytes=64)
        planes = [
            keep.tile([P, G, CHUNK], U8, name="plane%d" % c, align_bytes=64) for c in range(2)
        ]
        ident = keep.tile([P, P], BF16, name="ident")
        bias_rows = keep.tile([P, BLK], BF16, name="bias_rows")
        bias_all = keep.tile([P, NBLK * BLK], BF16, name="bias_all")
        cos_b = keep.tile([P, HALF], BF16, name="cos_b")
        sin_b = keep.tile([P, HALF], BF16, name="sin_b")
        cos4 = keep.tile([P, BLK], F32, name="cos4")
        sin4 = keep.tile([P, BLK], F32, name="sin4")
        cos2 = cos4[:, 0:HD]
        sin2 = sin4[:, 0:HD]
        wcs = [
            wpool.tile([P, G, 2 * CHUNK], U8, name="wc%d" % c, tag="wc", align_bytes=64)
            for c in range(4)
        ]

        def load_codes(c, blk0, nblk, g0, ng):
            col0 = c * CHUNK + blk0 * BLK
            nc.sync.dma_start(
                out=wcs[c][:, g0 : g0 + ng, 2 * blk0 * BLK : 2 * (blk0 + nblk) * BLK].bitcast(I32),
                in_=Wqk_words[g0 : g0 + ng, :, 2 * col0 : 2 * (col0 + nblk * BLK)]
                .rearrange("g p n -> p g n")
                .bitcast(I32),
            )

        def load_scales(c):
            cols = slice(c * CHUNK, (c + 1) * CHUNK)
            for q in range(2):
                for r in range(4):
                    nc.sync.dma_start(
                        out=planes[c % 2][32 * q + r : P : 64, :, :].bitcast(I32),
                        in_=Wqk_scales[:, 4 * q + r : 16 : 8, cols].rearrange("g q n -> q g n").bitcast(I32),
                    )

        def code_loads(c):
            todo = []
            for blk0, nblk, split in PLAN[c]:
                g0 = 0
                for ng in split:
                    todo.append((c, blk0, nblk, g0, ng))
                    g0 += ng
            return todo

        def spread_bias(j):
            bp = psum.tile([P, BLK], F32, name="bp%d" % j, tag="acc")
            nc.tensor.matmul(
                out=bp[:],
                lhsT=ident[:, j : j + 1].to_broadcast([P, P]),
                rhs=bias_rows[:],
                start=True,
                stop=True,
            )
            nc.scalar.copy(out=bias_all[:, j * BLK : (j + 1) * BLK], in_=bp[:])

        def epilogue(j, acc):
            t = work.tile([P, BLK], F32, name="t%d" % j, tag="t")
            u = work.tile([P, BLK], F32, name="u%d" % j, tag="u")
            w = work.tile([P, BLK], F32, name="w%d" % j, tag="w")
            o = work.tile([P, BLK], F32, name="o%d" % j, tag="o", bufs=12)
            for h in range(2):
                a = h * HD
                nc.vector.tensor_tensor(
                    out=t[:, a : a + HD],
                    in0=acc[:, a : a + HD],
                    in1=bias_all[:, j * BLK + a : j * BLK + a + HD],
                    op=ADD,
                )
            for h in range(2):
                a = h * HD
                nc.vector.tensor_tensor(out=u[:, a : a + HD], in0=t[:, a : a + HD], in1=cos2, op=MULT)
                nc.vector.tensor_tensor(out=w[:, a : a + HD], in0=t[:, a : a + HD], in1=sin2, op=MULT)
            for h in range(2):
                a = h * HD
                m = a + HALF
                nc.vector.tensor_tensor(out=o[:, a:m], in0=u[:, a:m], in1=w[:, m : a + HD], op=ADD)
                nc.vector.tensor_tensor(out=o[:, m : a + HD], in0=u[:, m : a + HD], in1=w[:, a:m], op=ADD)
            return o

        def epilogue_pair(j, acc_a, acc_b):
            tiles = []
            for i in range(2):
                tiles.append(
                    (
                        work.tile([P, BLK], F32, name="t%d" % (j + i), tag="t"),
                        work.tile([P, BLK], F32, name="u%d" % (j + i), tag="u"),
                        work.tile([P, BLK], F32, name="w%d" % (j + i), tag="w"),
                        work.tile([P, BLK], F32, name="o%d" % (j + i), tag="o", bufs=12),
                    )
                )
            for i, acc in enumerate((acc_a, acc_b)):
                nc.vector.tensor_tensor(
                    out=tiles[i][0][:],
                    in0=acc[:],
                    in1=bias_all[:, (j + i) * BLK : (j + i + 1) * BLK],
                    op=ADD,
                )
            for i in range(2):
                t, u, w, o = tiles[i]
                nc.vector.tensor_tensor(out=u[:], in0=t[:], in1=cos4[:], op=MULT)
                nc.vector.tensor_tensor(out=w[:], in0=t[:], in1=sin4[:], op=MULT)
            for i in range(2):
                t, u, w, o = tiles[i]
                o3 = o[:].rearrange("p (h f) -> p h f", h=2)
                u3 = u[:].rearrange("p (h f) -> p h f", h=2)
                w3 = w[:].rearrange("p (h f) -> p h f", h=2)
                nc.vector.tensor_tensor(out=o3[:, :, 0:HALF], in0=u3[:, :, 0:HALF], in1=w3[:, :, HALF:HD], op=ADD)
                nc.vector.tensor_tensor(out=o3[:, :, HALF:HD], in0=u3[:, :, HALF:HD], in1=w3[:, :, 0:HALF], op=ADD)
            return tiles[0][3], tiles[1][3]

        def store(j, o, b):
            dst = out_0 if j < 8 else out_1
            h0 = (j % 8) * 2
            nc.sync.dma_start(
                out=dst[b, h0 : h0 + 2, :, :].rearrange("h t f -> t h f"),
                in_=o[b:P:2, :].rearrange("p (h f) -> p h f", h=2),
            )

        nc.vector.memset(xs_raw[:].bitcast(I32), 0)
        nc.vector.memset(planes[0][:].bitcast(I32), 0)
        nc.vector.memset(planes[1][:].bitcast(I32), 0)
        nc.gpsimd.memset(bias_rows[:], 0.0)
        make_identity(nc, ident[:])

        first = code_loads(0)
        for g0, g1 in ((0, 3), (3, 6), (6, 8)):
            nc.sync.dma_start(
                out=x_raw[:, g0:g1, :].bitcast(I32),
                in_=x_words[g0:g1, :, :].rearrange("g p n -> p g n").bitcast(I32),
            )
        for r in range(4):
            nc.sync.dma_start(
                out=xs_raw[r:P:32, :, :].bitcast(I32),
                in_=x_scales[:, r:16:4, :].rearrange("g q n -> q g n").bitcast(I32),
            )
        load_codes(*first[0])
        load_codes(*first[1])
        load_scales(0)
        load_scales(1)
        nc.sync.dma_start(out=bias_rows[0:16, :], in_=bqk.rearrange("(j n) -> j n", j=16))
        for b in range(2):
            nc.sync.dma_start(out=cos_b[b:P:2, :], in_=cos)
            nc.sync.dma_start(out=sin_b[b:P:2, :], in_=sin)
        for args in first[2:] + code_loads(1):
            load_codes(*args)

        for g in range(G):
            nc.vector.tensor_copy(
                out=x_codes[:, g, :].rearrange("p (t b w) -> p t b w", b=2, w=2),
                in_=x_raw[:, g, :].rearrange("p (b t w) -> p t b w", b=2, w=2),
            )
        nc.vector.tensor_copy(
            out=xs[:].rearrange("p g (t b) -> p g t b", b=2),
            in_=xs_raw[:].rearrange("p g (b t) -> p g t b", b=2),
        )
        for a in range(0, BLK, HD):
            nc.gpsimd.tensor_copy(out=cos4[:, a : a + HALF], in_=cos_b[:])
            nc.gpsimd.tensor_copy(out=cos4[:, a + HALF : a + HD], in_=cos_b[:])
            nc.gpsimd.tensor_copy(out=sin4[:, a : a + HALF], in_=sin_b[:])
            nc.gpsimd.tensor_scalar(
                out=sin4[:, a + HALF : a + HD], in0=sin_b[:], scalar1=-1.0, scalar2=0.0, op0=MULT, op1=ADD
            )

        bias_todo = list(range(NBLK))
        waiting = []

        for c in range(4):
            for blk0, nblk, split in PLAN[c]:
                accs = [
                    psum.tile([P, BLK], F32, name="acc%d_%d" % (c, blk0 + i), tag="acc")
                    for i in range(nblk)
                ]
                g0 = 0
                for ng in split:
                    for i in range(nblk):
                        blk = blk0 + i
                        for g in range(g0, g0 + ng):
                            nc.tensor.matmul_mx(
                                out=accs[i][:],
                                lhsT=x_codes[:, g, :].bitcast(FP4X4),
                                lhsT_scale=xs[:, g, :],
                                rhs=wcs[c][:, g, 2 * blk * BLK : 2 * (blk + 1) * BLK].bitcast(FP4X4),
                                rhs_scale=planes[c % 2][:, g, blk * BLK : (blk + 1) * BLK],
                                start=(g == 0),
                                stop=(g == G - 1),
                            )
                    g0 += ng
                    for j in bias_todo[:4]:
                        spread_bias(j)
                    bias_todo = bias_todo[4:]
                j = c * 4 + blk0
                if c >= 2:
                    done = []
                    for i in range(0, nblk, 2):
                        done.extend(epilogue_pair(j + i, accs[i], accs[i + 1]))
                else:
                    done = [epilogue(j + i, accs[i]) for i in range(nblk)]
                for i in range(nblk):
                    waiting.extend([(j + i, done[i], 0), (j + i, done[i], 1)])
            if c < 2:
                load_scales(c + 2)
                for args in waiting[:FILL]:
                    store(*args)
                waiting = waiting[FILL:]
                for args in code_loads(c + 2):
                    load_codes(*args)
        for args in waiting:
            store(*args)
